import numpy as np
import ml_dtypes


def mxq(x, axis, fmt="e4m3"):
    dtype, down = {"e4m3": (ml_dtypes.float8_e4m3fn, 7), "e5m2": (ml_dtypes.float8_e5m2, 14)}[fmt]
    v = np.moveaxis(np.asarray(x, np.float32).astype(ml_dtypes.bfloat16).astype(np.float64), axis, -1)
    blocks = v.reshape(v.shape[:-1] + (-1, 32))
    amax = np.abs(blocks).max(-1, keepdims=True)
    byte = np.maximum(np.where(amax > 0, np.frexp(amax)[1] - 1 + 127, 0) - down, 1)
    scale = np.exp2(byte - 127.0)
    codes = (blocks / scale).astype(np.float32).astype(dtype).astype(np.float64)
    return np.moveaxis((codes * scale).reshape(v.shape), -1, axis)


WIDE = False


def mx_kscale(k):
    if not WIDE:
        return np.ones(k)
    levels = np.array([10, -10, 5, -5, 0])
    a = np.random.permutation(np.resize(levels, k // 512 * 4)).reshape(k // 512, 4)
    idx = np.arange(k)
    return np.exp2(a[idx // 512, idx % 128 // 32])


BF16 = ml_dtypes.bfloat16


def bf(x):
    return np.asarray(x, np.float32).astype(BF16)


def f64(x):
    return np.asarray(x).astype(np.float64)


B, P, C, HS, NG = 8, 512, 768, 512, 2
GMIN, GMAX = -1.0, 1.0


def silu(v):
    return v / (1.0 + np.exp(-v))


def rbf(v):
    grid = np.linspace(GMIN, GMAX, NG)
    denom = (GMAX - GMIN) / (NG - 1)
    return np.exp(-np.square((v[..., None] - grid) / denom))


def setup_inputs():
    s = mx_kscale(P * NG)[::NG]
    u = s / s.max()
    r = np.sqrt(np.log(1.0 / u))
    d = (GMAX - GMIN) / (NG - 1)
    m = (GMAX + d * r) * (r > 0)
    return {"x": bf(np.random.standard_normal((B, P, C)) * (d / (d + 2.0 * r))[:, None] + m[:, None]),
            "fc1_spline_w": bf(np.random.standard_normal((HS, P * NG)) * 0.7 / np.sqrt(P) / np.repeat(u, NG)),
            "fc1_base_w": bf(np.random.standard_normal((HS, P)) / np.sqrt(P) / (1.0 + m)),
            "fc1_base_b": bf(np.random.standard_normal(HS) * 0.1)}


def reference(x, fc1_spline_w, fc1_base_w, fc1_base_b):
    h = np.swapaxes(f64(x), 1, 2)
    basis = rbf(h).reshape(B, C, P * NG)
    out = mxq(basis, 2, "e4m3") @ mxq(f64(fc1_spline_w).T, 0, "e4m3")
    out = out + (mxq(silu(h), 2, "e4m3") @ mxq(f64(fc1_base_w).T, 0, "e4m3")) + f64(fc1_base_b)
    return out

@@ -1,0 +1,248 @@
+from contextlib import ExitStack
+
+import concourse.mybir as mybir
+from concourse.masks import make_identity
+
+F32 = mybir.dt.float32
+BF16 = mybir.dt.bfloat16
+U32 = mybir.dt.uint32
+U8 = mybir.dt.uint8
+FP8X4 = mybir.dt.float8_e4m3fn_x4
+FUNC = mybir.ActivationFunctionType
+ALU = mybir.AluOpType
+
+BATCH, PATCHES, CHANNELS, OUTS = 8, 512, 768, 512
+P = 128
+PACK = 4
+ROWS = PATCHES // P
+UNIT_C = 256
+C_TILES = UNIT_C // P
+UNITS_PER_BATCH = CHANNELS // UNIT_C
+UNITS = BATCH * UNITS_PER_BATCH
+SPLINE_PASSES = 2
+BASE_PASS = 2
+WEIGHT_PASSES = SPLINE_PASSES + 1
+LEAD = 6
+FIRST_WEIGHT_BATCH = BATCH - WEIGHT_PASSES
+
+FLOPS = 2 * BATCH * CHANNELS * OUTS * (2 * PATCHES + PATCHES)
+
+
+def tile_kan1_pa_t_kernel(tc, x, fc1_spline_w, fc1_base_w, fc1_base_b, out):
+    nc = tc.nc
+    with ExitStack() as ctx:
+        keep = ctx.enter_context(tc.tile_pool(name="keep", bufs=1))
+        silu_pool = ctx.enter_context(tc.tile_pool(name="silu_pool", bufs=6))
+        square_pool = ctx.enter_context(tc.tile_pool(name="square_pool", bufs=LEAD + 1))
+        basis_pool = ctx.enter_context(tc.tile_pool(name="basis_pool", bufs=3))
+        result_pool = ctx.enter_context(tc.tile_pool(name="result_pool", bufs=6))
+        psum_w = ctx.enter_context(tc.psum_pool(name="psum_w", bufs=2))
+        psum_acc = ctx.enter_context(tc.psum_pool(name="psum_acc", bufs=6))
+        ctx.enter_context(tc.manual_schedule())
+
+        x_sb = [keep.tile([P, ROWS * CHANNELS], BF16, name="x_sb%d" % b) for b in range(BATCH)]
+        ws_raw = keep.tile([P, 4 * 2 * PATCHES], BF16)
+        wb_raw = keep.tile([P, 4 * PATCHES], BF16)
+        w_grouped = keep.tile([P, WEIGHT_PASSES * OUTS * PACK], BF16, align_bytes=64)
+        w_codes = keep.tile([P, WEIGHT_PASSES * OUTS], U32, align_bytes=64)
+        w_scales = keep.tile([P, WEIGHT_PASSES * OUTS], U8, align_bytes=64)
+        silu_codes = keep.tile([P, UNITS * UNIT_C], U32, align_bytes=64)
+        silu_scales = keep.tile([P, UNITS * UNIT_C], U8, align_bytes=64)
+        bias_bf = keep.tile([P, OUTS], BF16)
+        bias_f32 = keep.tile([P, OUTS], F32)
+        identity = keep.tile([P, P], F32)
+        minus_quarter = keep.tile([P, 1], F32)
+        plus_one = keep.tile([P, 1], F32)
+        minus_one = keep.tile([P, 1], F32)
+        warm = keep.tile([P, 1], F32)
+
+        def x_block(n):
+            b, cb = divmod(n, UNITS_PER_BATCH)
+            rows = x_sb[b][:].rearrange("q (r c) -> q r c", r=ROWS)
+            return rows[:, :, cb * UNIT_C : (cb + 1) * UNIT_C]
+
+        def load_x(b):
+            nc.sync.dma_start(
+                out=x_sb[b][:].rearrange("q (g r) -> q g r", g=2),
+                in_=x[b].rearrange("(g q j) c -> q g (j c)", g=2, j=2),
+            )
+
+        def load_x_block(n):
+            b, cb = divmod(n, UNITS_PER_BATCH)
+            for g in range(2):
+                nc.sync.dma_start(
+                    out=x_block(n)[:, 2 * g : 2 * g + 2, :],
+                    in_=x[b, g * 2 * P : (g + 1) * 2 * P, cb * UNIT_C : (cb + 1) * UNIT_C].rearrange(
+                        "(q j) c -> q j c", j=2
+                    ),
+                )
+
+        def silu(n):
+            silu_bf = silu_pool.tile([P, UNIT_C * PACK], BF16, align_bytes=64)
+            nc.scalar.activation(
+                out=silu_bf[:].rearrange("q (s i r) -> q s r i", i=4, r=ROWS),
+                in_=x_block(n).rearrange("q r (s i) -> q s r i", i=4),
+                func=FUNC.Silu,
+            )
+            return silu_bf
+
+        def quantise_silu(n, silu_bf):
+            cols = slice(n * UNIT_C, (n + 1) * UNIT_C)
+            nc.vector.quantize_mx(
+                out=silu_codes[:, cols].bitcast(FP8X4), scales=silu_scales[:, cols], in_=silu_bf[:]
+            )
+
+        def scalar_squares(n):
+            return n >= LEAD and n % UNITS_PER_BATCH == UNITS_PER_BATCH - 1
+
+        def square(n):
+            squares = square_pool.tile([P, ROWS * 2 * UNIT_C], F32)
+            planes = squares[:].rearrange("q (r i c) -> q r i c", r=ROWS, i=2)
+            if scalar_squares(n):
+                for i, shift in enumerate((plus_one, minus_one)):
+                    nc.scalar.activation(
+                        out=planes[:, :, i, :], in_=x_block(n), func=FUNC.Square, bias=shift[:], scale=1.0
+                    )
+            else:
+                for i, shift in enumerate((2.0, -2.0)):
+                    nc.vector.scalar_tensor_tensor(
+                        out=planes[:, :, i, :],
+                        in0=x_block(n),
+                        scalar=shift,
+                        in1=x_block(n),
+                        op0=ALU.add,
+                        op1=ALU.mult,
+                    )
+            return squares
+
+        def exp_basis(n, squares):
+            basis_bf = basis_pool.tile([P, SPLINE_PASSES * UNIT_C * PACK], BF16, align_bytes=64)
+            src = squares[:].rearrange("q (g t s i) -> q g s t i", g=SPLINE_PASSES, t=PACK, i=4)
+            dst = basis_bf[:].rearrange("q (g s i t) -> q g s t i", g=SPLINE_PASSES, t=PACK, i=4)
+            for g in range(SPLINE_PASSES):
+                if scalar_squares(n):
+                    nc.scalar.activation(out=dst[:, g], in_=src[:, g], func=FUNC.Exp, scale=-0.25)
+                else:
+                    nc.scalar.activation(
+                        out=dst[:, g], in_=src[:, g], func=FUNC.Exp, scale=-0.25, bias=minus_quarter[:]
+                    )
+            return basis_bf
+
+        def quantise_basis(basis_bf):
+            basis_codes = basis_pool.tile([P, SPLINE_PASSES * UNIT_C], U32, align_bytes=64)
+            basis_scales = basis_pool.tile([P, SPLINE_PASSES * UNIT_C], U8, align_bytes=64)
+            for g in range(SPLINE_PASSES):
+                cols = slice(g * UNIT_C, (g + 1) * UNIT_C)
+                nc.vector.quantize_mx(
+                    out=basis_codes[:, cols].bitcast(FP8X4),
+                    scales=basis_scales[:, cols],
+                    in_=basis_bf[:, g * UNIT_C * PACK : (g + 1) * UNIT_C * PACK],
+                )
+            return basis_codes, basis_scales
+
+        def weight_pass(w):
+            cols = slice(w * OUTS, (w + 1) * OUTS)
+            return w_codes[:, cols].bitcast(FP8X4), w_scales[:, cols]
+
+        def multiply(n, basis_codes, basis_scales):
+            sums = [psum_acc.tile([P, OUTS], F32, name="acc%d" % ct, tag="acc") for ct in range(C_TILES)]
+            rhs, rhs_scale = weight_pass(BASE_PASS)
+            for ct in range(C_TILES):
+                cols = slice(n * UNIT_C + ct * P, n * UNIT_C + (ct + 1) * P)
+                nc.tensor.matmul_mx(
+                    out=sums[ct][:],
+                    lhsT=silu_codes[:, cols].bitcast(FP8X4),
+                    lhsT_scale=silu_scales[:, cols],
+                    rhs=rhs,
+                    rhs_scale=rhs_scale,
+                    start=True,
+                    stop=False,
+                )
+            for g in range(SPLINE_PASSES):
+                rhs, rhs_scale = weight_pass(g)
+                for ct in range(C_TILES):
+                    cols = slice(g * UNIT_C + ct * P, g * UNIT_C + (ct + 1) * P)
+                    nc.tensor.matmul_mx(
+                        out=sums[ct][:],
+                        lhsT=basis_codes[:, cols].bitcast(FP8X4),
+                        lhsT_scale=basis_scales[:, cols],
+                        rhs=rhs,
+                        rhs_scale=rhs_scale,
+                        start=False,
+                        stop=(g == SPLINE_PASSES - 1),
+                    )
+            return sums
+
+        def add_bias_and_store(n, sums):
+            b, cb = divmod(n, UNITS_PER_BATCH)
+            for ct in range(C_TILES):
+                result = result_pool.tile([P, OUTS], F32)
+                nc.vector.tensor_tensor(out=result[:], in0=sums[ct][:], in1=bias_f32[:], op=ALU.add)
+                first = cb * UNIT_C + ct * P
+                nc.sync.dma_start(out=out[b, first : first + P, :], in_=result[:])
+
+        def prepare_weights(w):
+            grouped_words = w_grouped[:].bitcast(F32).rearrange("q (w o u) -> q w o u", w=WEIGHT_PASSES, u=2)
+            if w == BASE_PASS:
+                words = wb_raw[:].bitcast(F32).rearrange("o (ob k) -> o ob k", ob=4)
+            else:
+                words = ws_raw[:].bitcast(F32).rearrange("o (ob k) -> o ob k", ob=4)
+            for half in range(2):
+                bank = psum_w.tile([P, 2, 2 * P], F32)
+                for u in range(2):
+                    if w == BASE_PASS:
+                        picked = slice(u * P, (u + 1) * P)
+                    else:
+                        picked = slice(w * 2 * P + u, (w + 1) * 2 * P, 2)
+                    for ob in range(2):
+                        nc.tensor.transpose(
+                            bank[:, u, ob * P : (ob + 1) * P], words[:, 2 * half + ob, picked], identity[:]
+                        )
+                nc.vector.tensor_copy(
+                    out=grouped_words[:, w, half * 2 * P : (half + 1) * 2 * P, :],
+                    in_=bank[:].rearrange("q u o -> q o u"),
+                )
+            codes, scales = weight_pass(w)
+            nc.vector.quantize_mx(
+                out=codes, scales=scales, in_=w_grouped[:, w * OUTS * PACK : (w + 1) * OUTS * PACK]
+            )
+
+        nc.vector.memset(minus_quarter[:], -0.25)
+        nc.vector.memset(plus_one[:], 1.0)
+        nc.vector.memset(minus_one[:], -1.0)
+        nc.scalar.activation(out=warm[:], in_=minus_quarter[:], func=FUNC.Silu)
+        make_identity(nc, identity[:])
+
+        for n in range(UNITS_PER_BATCH):
+            load_x_block(n)
+        for b in range(1, BATCH):
+            load_x(b)
+        nc.sync.dma_start(out=ws_raw[:].rearrange("o (ob k) -> o ob k", ob=4),
+                          in_=fc1_spline_w.rearrange("(ob o) k -> o ob k", o=P))
+        nc.sync.dma_start(out=wb_raw[:].rearrange("o (ob k) -> o ob k", ob=4),
+                          in_=fc1_base_w.rearrange("(ob o) k -> o ob k", o=P))
+        nc.sync.dma_start(out=bias_bf[:], in_=fc1_base_b.partition_broadcast(P))
+
+        squares_of = {}
+        for b in range(BATCH):
+            units = range(b * UNITS_PER_BATCH, (b + 1) * UNITS_PER_BATCH)
+            silu_tiles = [silu(n) for n in units]
+            if b < LEAD:
+                squares_of[b] = square(b)
+            if b >= FIRST_WEIGHT_BATCH:
+                prepare_weights(b - FIRST_WEIGHT_BATCH)
+            for n, silu_bf in zip(units, silu_tiles):
+                quantise_silu(n, silu_bf)
+        nc.vector.tensor_copy(out=bias_f32[:], in_=bias_bf[:])
+
+        waiting = None
+        for n in range(UNITS):
+            if n + LEAD < UNITS:
+                squares_of[n + LEAD] = square(n + LEAD)
+            basis_bf = exp_basis(n, squares_of[n])
+            basis_codes, basis_scales = quantise_basis(basis_bf)
+            sums = multiply(n, basis_codes, basis_scales)
+            if waiting is not None:
+                add_bias_and_store(n - 1, waiting)
+            waiting = sums
+        add_bias_and_store(UNITS - 1, waiting)

@@ -32,8 +32,9 @@ def tile_kan1_pa_t_kernel(tc, x, fc1_spline_w, fc1_base_w, fc1_base_b, out):
     nc = tc.nc
     with ExitStack() as ctx:
         keep = ctx.enter_context(tc.tile_pool(name="keep", bufs=1))
-        silu_pool = ctx.enter_context(tc.tile_pool(name="silu_pool", bufs=6))
+        silu_pool = ctx.enter_context(tc.tile_pool(name="silu_pool", bufs=3))
         square_pool = ctx.enter_context(tc.tile_pool(name="square_pool", bufs=LEAD + 1))
+        shifted_pool = ctx.enter_context(tc.tile_pool(name="shifted_pool", bufs=2))
         basis_pool = ctx.enter_context(tc.tile_pool(name="basis_pool", bufs=3))
         result_pool = ctx.enter_context(tc.tile_pool(name="result_pool", bufs=6))
         psum_w = ctx.enter_context(tc.psum_pool(name="psum_w", bufs=2))
@@ -52,8 +53,6 @@ def tile_kan1_pa_t_kernel(tc, x, fc1_spline_w, fc1_base_w, fc1_base_b, out):
         bias_f32 = keep.tile([P, OUTS], F32)
         identity = keep.tile([P, P], F32)
         minus_quarter = keep.tile([P, 1], F32)
-        plus_one = keep.tile([P, 1], F32)
-        minus_one = keep.tile([P, 1], F32)
         warm = keep.tile([P, 1], F32)
 
         def x_block(n):
@@ -77,34 +76,36 @@ def tile_kan1_pa_t_kernel(tc, x, fc1_spline_w, fc1_base_w, fc1_base_b, out):
                     ),
                 )
 
-        def silu(n):
-            silu_bf = silu_pool.tile([P, UNIT_C * PACK], BF16, align_bytes=64)
+        def silu(b, silu_bf, first, width):
+            rows = x_sb[b][:].rearrange("q (r c) -> q r c", r=ROWS)[:, :, first : first + width]
             nc.scalar.activation(
-                out=silu_bf[:].rearrange("q (s i r) -> q s r i", i=4, r=ROWS),
-                in_=x_block(n).rearrange("q r (s i) -> q s r i", i=4),
+                out=silu_bf[:, first * PACK : (first + width) * PACK].rearrange("q (s i r) -> q s r i", i=4, r=ROWS),
+                in_=rows.rearrange("q r (s i) -> q s r i", i=4),
                 func=FUNC.Silu,
             )
-            return silu_bf
 
-        def quantise_silu(n, silu_bf):
-            cols = slice(n * UNIT_C, (n + 1) * UNIT_C)
+        def quantise_silu(b, silu_bf, first, width):
+            cols = slice(b * CHANNELS + first, b * CHANNELS + first + width)
             nc.vector.quantize_mx(
-                out=silu_codes[:, cols].bitcast(FP8X4), scales=silu_scales[:, cols], in_=silu_bf[:]
+                out=silu_codes[:, cols].bitcast(FP8X4),
+                scales=silu_scales[:, cols],
+                in_=silu_bf[:, first * PACK : (first + width) * PACK],
             )
 
-        def scalar_squares(n):
-            return n >= LEAD and n % UNITS_PER_BATCH == UNITS_PER_BATCH - 1
+        def gpsimd_squares(n):
+            return n % 4 != 3
 
         def square(n):
             squares = square_pool.tile([P, ROWS * 2 * UNIT_C], F32)
             planes = squares[:].rearrange("q (r i c) -> q r i c", r=ROWS, i=2)
-            if scalar_squares(n):
-                for i, shift in enumerate((plus_one, minus_one)):
-                    nc.scalar.activation(
-                        out=planes[:, :, i, :], in_=x_block(n), func=FUNC.Square, bias=shift[:], scale=1.0
+            for i, shift in enumerate((2.0, -2.0)):
+                if i == 1 and gpsimd_squares(n):
+                    shifted = shifted_pool.tile([P, ROWS, UNIT_C], F32)
+                    nc.gpsimd.tensor_scalar(
+                        out=shifted[:], in0=x_block(n), scalar1=1.0, scalar2=shift, op0=ALU.mult, op1=ALU.add
                     )
-            else:
-                for i, shift in enumerate((2.0, -2.0)):
+                    nc.gpsimd.tensor_tensor(out=planes[:, :, i, :], in0=shifted[:], in1=x_block(n), op=ALU.mult)
+                else:
                     nc.vector.scalar_tensor_tensor(
                         out=planes[:, :, i, :],
                         in0=x_block(n),
@@ -115,29 +116,20 @@ def tile_kan1_pa_t_kernel(tc, x, fc1_spline_w, fc1_base_w, fc1_base_b, out):
                     )
             return squares
 
-        def exp_basis(n, squares):
+        def exp_basis(squares):
             basis_bf = basis_pool.tile([P, SPLINE_PASSES * UNIT_C * PACK], BF16, align_bytes=64)
             src = squares[:].rearrange("q (g t s i) -> q g s t i", g=SPLINE_PASSES, t=PACK, i=4)
             dst = basis_bf[:].rearrange("q (g s i t) -> q g s t i", g=SPLINE_PASSES, t=PACK, i=4)
             for g in range(SPLINE_PASSES):
-                if scalar_squares(n):
-                    nc.scalar.activation(out=dst[:, g], in_=src[:, g], func=FUNC.Exp, scale=-0.25)
-                else:
-                    nc.scalar.activation(
-                        out=dst[:, g], in_=src[:, g], func=FUNC.Exp, scale=-0.25, bias=minus_quarter[:]
-                    )
+                nc.scalar.activation(
+                    out=dst[:, g], in_=src[:, g], func=FUNC.Exp, scale=-0.25, bias=minus_quarter[:]
+                )
             return basis_bf
 
         def quantise_basis(basis_bf):
             basis_codes = basis_pool.tile([P, SPLINE_PASSES * UNIT_C], U32, align_bytes=64)
             basis_scales = basis_pool.tile([P, SPLINE_PASSES * UNIT_C], U8, align_bytes=64)
-            for g in range(SPLINE_PASSES):
-                cols = slice(g * UNIT_C, (g + 1) * UNIT_C)
-                nc.vector.quantize_mx(
-                    out=basis_codes[:, cols].bitcast(FP8X4),
-                    scales=basis_scales[:, cols],
-                    in_=basis_bf[:, g * UNIT_C * PACK : (g + 1) * UNIT_C * PACK],
-                )
+            nc.vector.quantize_mx(out=basis_codes[:].bitcast(FP8X4), scales=basis_scales[:], in_=basis_bf[:])
             return basis_codes, basis_scales
 
         def weight_pass(w):
@@ -208,8 +200,6 @@ def tile_kan1_pa_t_kernel(tc, x, fc1_spline_w, fc1_base_w, fc1_base_b, out):
             )
 
         nc.vector.memset(minus_quarter[:], -0.25)
-        nc.vector.memset(plus_one[:], 1.0)
-        nc.vector.memset(minus_one[:], -1.0)
         nc.scalar.activation(out=warm[:], in_=minus_quarter[:], func=FUNC.Silu)
         make_identity(nc, identity[:])
 
@@ -225,21 +215,22 @@ def tile_kan1_pa_t_kernel(tc, x, fc1_spline_w, fc1_base_w, fc1_base_b, out):
 
         squares_of = {}
         for b in range(BATCH):
-            units = range(b * UNITS_PER_BATCH, (b + 1) * UNITS_PER_BATCH)
-            silu_tiles = [silu(n) for n in units]
+            silu_bf = silu_pool.tile([P, CHANNELS * PACK], BF16, align_bytes=64)
+            for first in range(0, CHANNELS, UNIT_C if b == 0 else CHANNELS):
+                silu(b, silu_bf, first, UNIT_C if b == 0 else CHANNELS)
             if b < LEAD:
                 squares_of[b] = square(b)
             if b >= FIRST_WEIGHT_BATCH:
                 prepare_weights(b - FIRST_WEIGHT_BATCH)
-            for n, silu_bf in zip(units, silu_tiles):
-                quantise_silu(n, silu_bf)
+            quantise_silu(b, silu_bf, 0, 2 * UNIT_C)
+            quantise_silu(b, silu_bf, 2 * UNIT_C, UNIT_C)
         nc.vector.tensor_copy(out=bias_f32[:], in_=bias_bf[:])
 
         waiting = None
         for n in range(UNITS):
             if n + LEAD < UNITS:
                 squares_of[n + LEAD] = square(n + LEAD)
-            basis_bf = exp_basis(n, squares_of[n])
+            basis_bf = exp_basis(squares_of[n])
             basis_codes, basis_scales = quantise_basis(basis_bf)
             sums = multiply(n, basis_codes, basis_scales)
             if waiting is not None:

@@ -22,7 +22,7 @@ UNITS = BATCH * UNITS_PER_BATCH
 SPLINE_PASSES = 2
 BASE_PASS = 2
 WEIGHT_PASSES = SPLINE_PASSES + 1
-LEAD = 6
+LEAD = 9
 FIRST_WEIGHT_BATCH = BATCH - WEIGHT_PASSES
 
 FLOPS = 2 * BATCH * CHANNELS * OUTS * (2 * PATCHES + PATCHES)
@@ -32,12 +32,11 @@ def tile_kan1_pa_t_kernel(tc, x, fc1_spline_w, fc1_base_w, fc1_base_b, out):
     nc = tc.nc
     with ExitStack() as ctx:
         keep = ctx.enter_context(tc.tile_pool(name="keep", bufs=1))
-        silu_pool = ctx.enter_context(tc.tile_pool(name="silu_pool", bufs=3))
+        silu_pool = ctx.enter_context(tc.tile_pool(name="silu_pool", bufs=2))
         square_pool = ctx.enter_context(tc.tile_pool(name="square_pool", bufs=LEAD + 1))
-        shifted_pool = ctx.enter_context(tc.tile_pool(name="shifted_pool", bufs=2))
         basis_pool = ctx.enter_context(tc.tile_pool(name="basis_pool", bufs=3))
-        result_pool = ctx.enter_context(tc.tile_pool(name="result_pool", bufs=6))
-        psum_w = ctx.enter_context(tc.psum_pool(name="psum_w", bufs=2))
+        result_pool = ctx.enter_context(tc.tile_pool(name="result_pool", bufs=4))
+        psum_quarter = ctx.enter_context(tc.psum_pool(name="psum_quarter", bufs=2))
         psum_acc = ctx.enter_context(tc.psum_pool(name="psum_acc", bufs=6))
         ctx.enter_context(tc.manual_schedule())
 
@@ -52,6 +51,7 @@ def tile_kan1_pa_t_kernel(tc, x, fc1_spline_w, fc1_base_w, fc1_base_b, out):
         bias_bf = keep.tile([P, OUTS], BF16)
         bias_f32 = keep.tile([P, OUTS], F32)
         identity = keep.tile([P, P], F32)
+        quarter_identity = keep.tile([P, P], BF16)
         minus_quarter = keep.tile([P, 1], F32)
         warm = keep.tile([P, 1], F32)
 
@@ -92,28 +92,22 @@ def tile_kan1_pa_t_kernel(tc, x, fc1_spline_w, fc1_base_w, fc1_base_b, out):
                 in_=silu_bf[:, first * PACK : (first + width) * PACK],
             )
 
-        def gpsimd_squares(n):
-            return n % 4 != 3
+        def quarter(n):
+            bank = psum_quarter.tile([P, ROWS, UNIT_C], BF16)
+            for half in range(2):
+                rows = slice(2 * half, 2 * half + 2)
+                nc.tensor.matmul(
+                    out=bank[:, rows, :], lhsT=quarter_identity[:], rhs=x_block(n)[:, rows, :], start=True, stop=True
+                )
+            return bank
 
-        def square(n):
+        def square(n, bank):
             squares = square_pool.tile([P, ROWS * 2 * UNIT_C], F32)
             planes = squares[:].rearrange("q (r i c) -> q r i c", r=ROWS, i=2)
-            for i, shift in enumerate((2.0, -2.0)):
-                if i == 1 and gpsimd_squares(n):
-                    shifted = shifted_pool.tile([P, ROWS, UNIT_C], F32)
-                    nc.gpsimd.tensor_scalar(
-                        out=shifted[:], in0=x_block(n), scalar1=1.0, scalar2=shift, op0=ALU.mult, op1=ALU.add
-                    )
-                    nc.gpsimd.tensor_tensor(out=planes[:, :, i, :], in0=shifted[:], in1=x_block(n), op=ALU.mult)
-                else:
-                    nc.vector.scalar_tensor_tensor(
-                        out=planes[:, :, i, :],
-                        in0=x_block(n),
-                        scalar=shift,
-                        in1=x_block(n),
-                        op0=ALU.add,
-                        op1=ALU.mult,
-                    )
+            nc.vector.scalar_tensor_tensor(
+                out=planes[:, :, 0, :], in0=x_block(n), scalar=2.0, in1=bank[:], op0=ALU.add, op1=ALU.mult
+            )
+            nc.gpsimd.tensor_tensor(out=planes[:, :, 1, :], in0=planes[:, :, 0, :], in1=x_block(n), op=ALU.subtract)
             return squares
 
         def exp_basis(squares):
@@ -122,7 +116,7 @@ def tile_kan1_pa_t_kernel(tc, x, fc1_spline_w, fc1_base_w, fc1_base_b, out):
             dst = basis_bf[:].rearrange("q (g s i t) -> q g s t i", g=SPLINE_PASSES, t=PACK, i=4)
             for g in range(SPLINE_PASSES):
                 nc.scalar.activation(
-                    out=dst[:, g], in_=src[:, g], func=FUNC.Exp, scale=-0.25, bias=minus_quarter[:]
+                    out=dst[:, g], in_=src[:, g], func=FUNC.Exp, scale=-1.0, bias=minus_quarter[:]
                 )
             return basis_bf
 
@@ -180,7 +174,7 @@ def tile_kan1_pa_t_kernel(tc, x, fc1_spline_w, fc1_base_w, fc1_base_b, out):
             else:
                 words = ws_raw[:].bitcast(F32).rearrange("o (ob k) -> o ob k", ob=4)
             for half in range(2):
-                bank = psum_w.tile([P, 2, 2 * P], F32)
+                bank = psum_acc.tile([P, 2, 2 * P], F32, name="w_bank", tag="acc")
                 for u in range(2):
                     if w == BASE_PASS:
                         picked = slice(u * P, (u + 1) * P)
@@ -202,6 +196,9 @@ def tile_kan1_pa_t_kernel(tc, x, fc1_spline_w, fc1_base_w, fc1_base_b, out):
         nc.vector.memset(minus_quarter[:], -0.25)
         nc.scalar.activation(out=warm[:], in_=minus_quarter[:], func=FUNC.Silu)
         make_identity(nc, identity[:])
+        nc.vector.tensor_scalar(
+            out=quarter_identity[:], in0=identity[:], scalar1=0.25, scalar2=None, op0=ALU.mult
+        )
 
         for n in range(UNITS_PER_BATCH):
             load_x_block(n)
@@ -214,22 +211,30 @@ def tile_kan1_pa_t_kernel(tc, x, fc1_spline_w, fc1_base_w, fc1_base_b, out):
         nc.sync.dma_start(out=bias_bf[:], in_=fc1_base_b.partition_broadcast(P))
 
         squares_of = {}
-        for b in range(BATCH):
-            silu_bf = silu_pool.tile([P, CHANNELS * PACK], BF16, align_bytes=64)
+        quarters = {n: quarter(n) for n in range(2)}
+        silu_waiting = None
+        for b in range(BATCH + 1):
+            for n in range(b * LEAD // BATCH, min((b + 1) * LEAD // BATCH, LEAD)):
+                squares_of[n] = square(n, quarters[n])
+                quarters[n + 2] = quarter(n + 2)
+            if silu_waiting is not None:
+                quantise_silu(b - 1, silu_waiting, 0, 2 * UNIT_C)
+                quantise_silu(b - 1, silu_waiting, 2 * UNIT_C, UNIT_C)
+            if b == BATCH:
+                break
+            silu_waiting = silu_pool.tile([P, CHANNELS * PACK], BF16, align_bytes=64)
             for first in range(0, CHANNELS, UNIT_C if b == 0 else CHANNELS):
-                silu(b, silu_bf, first, UNIT_C if b == 0 else CHANNELS)
-            if b < LEAD:
-                squares_of[b] = square(b)
+                silu(b, silu_waiting, first, UNIT_C if b == 0 else CHANNELS)
             if b >= FIRST_WEIGHT_BATCH:
                 prepare_weights(b - FIRST_WEIGHT_BATCH)
-            quantise_silu(b, silu_bf, 0, 2 * UNIT_C)
-            quantise_silu(b, silu_bf, 2 * UNIT_C, UNIT_C)
         nc.vector.tensor_copy(out=bias_f32[:], in_=bias_bf[:])
 
         waiting = None
         for n in range(UNITS):
             if n + LEAD < UNITS:
-                squares_of[n + LEAD] = square(n + LEAD)
+                squares_of[n + LEAD] = square(n + LEAD, quarters[n + LEAD])
+            if n + LEAD + 2 < UNITS:
+                quarters[n + LEAD + 2] = quarter(n + LEAD + 2)
             basis_bf = exp_basis(squares_of[n])
             basis_codes, basis_scales = quantise_basis(basis_bf)
             sums = multiply(n, basis_codes, basis_scales)

@@ -22,8 +22,8 @@ UNITS = BATCH * UNITS_PER_BATCH
 SPLINE_PASSES = 2
 BASE_PASS = 2
 WEIGHT_PASSES = SPLINE_PASSES + 1
-LEAD = 9
-FIRST_WEIGHT_BATCH = BATCH - WEIGHT_PASSES
+LEAD = 11
+FIRST_WEIGHT_BATCH = 4
 
 FLOPS = 2 * BATCH * CHANNELS * OUTS * (2 * PATCHES + PATCHES)
 
@@ -32,7 +32,8 @@ def tile_kan1_pa_t_kernel(tc, x, fc1_spline_w, fc1_base_w, fc1_base_b, out):
     nc = tc.nc
     with ExitStack() as ctx:
         keep = ctx.enter_context(tc.tile_pool(name="keep", bufs=1))
-        silu_pool = ctx.enter_context(tc.tile_pool(name="silu_pool", bufs=2))
+        bf16_pool = ctx.enter_context(tc.tile_pool(name="bf16_pool", bufs=3))
+        weight_pool = ctx.enter_context(tc.tile_pool(name="weight_pool", bufs=1))
         square_pool = ctx.enter_context(tc.tile_pool(name="square_pool", bufs=LEAD + 1))
         basis_pool = ctx.enter_context(tc.tile_pool(name="basis_pool", bufs=3))
         result_pool = ctx.enter_context(tc.tile_pool(name="result_pool", bufs=4))
@@ -43,7 +44,6 @@ def tile_kan1_pa_t_kernel(tc, x, fc1_spline_w, fc1_base_w, fc1_base_b, out):
         x_sb = [keep.tile([P, ROWS * CHANNELS], BF16, name="x_sb%d" % b) for b in range(BATCH)]
         ws_raw = keep.tile([P, 4 * 2 * PATCHES], BF16)
         wb_raw = keep.tile([P, 4 * PATCHES], BF16)
-        w_grouped = keep.tile([P, WEIGHT_PASSES * OUTS * PACK], BF16, align_bytes=64)
         w_codes = keep.tile([P, WEIGHT_PASSES * OUTS], U32, align_bytes=64)
         w_scales = keep.tile([P, WEIGHT_PASSES * OUTS], U8, align_bytes=64)
         silu_codes = keep.tile([P, UNITS * UNIT_C], U32, align_bytes=64)
@@ -111,7 +111,7 @@ def tile_kan1_pa_t_kernel(tc, x, fc1_spline_w, fc1_base_w, fc1_base_b, out):
             return squares
 
         def exp_basis(squares):
-            basis_bf = basis_pool.tile([P, SPLINE_PASSES * UNIT_C * PACK], BF16, align_bytes=64)
+            basis_bf = bf16_pool.tile([P, SPLINE_PASSES * UNIT_C * PACK], BF16, name="basis_bf", tag="bf16", align_bytes=64)
             src = squares[:].rearrange("q (g t s i) -> q g s t i", g=SPLINE_PASSES, t=PACK, i=4)
             dst = basis_bf[:].rearrange("q (g s i t) -> q g s t i", g=SPLINE_PASSES, t=PACK, i=4)
             for g in range(SPLINE_PASSES):
@@ -167,14 +167,14 @@ def tile_kan1_pa_t_kernel(tc, x, fc1_spline_w, fc1_base_w, fc1_base_b, out):
                 first = cb * UNIT_C + ct * P
                 nc.sync.dma_start(out=out[b, first : first + P, :], in_=result[:])
 
-        def prepare_weights(w):
-            grouped_words = w_grouped[:].bitcast(F32).rearrange("q (w o u) -> q w o u", w=WEIGHT_PASSES, u=2)
+        def transpose_weights(w):
             if w == BASE_PASS:
                 words = wb_raw[:].bitcast(F32).rearrange("o (ob k) -> o ob k", ob=4)
             else:
                 words = ws_raw[:].bitcast(F32).rearrange("o (ob k) -> o ob k", ob=4)
+            banks = []
             for half in range(2):
-                bank = psum_acc.tile([P, 2, 2 * P], F32, name="w_bank", tag="acc")
+                bank = psum_acc.tile([P, 2, 2 * P], F32, name="w_bank%d" % half, tag="acc")
                 for u in range(2):
                     if w == BASE_PASS:
                         picked = slice(u * P, (u + 1) * P)
@@ -184,14 +184,19 @@ def tile_kan1_pa_t_kernel(tc, x, fc1_spline_w, fc1_base_w, fc1_base_b, out):
                         nc.tensor.transpose(
                             bank[:, u, ob * P : (ob + 1) * P], words[:, 2 * half + ob, picked], identity[:]
                         )
+                banks.append(bank)
+            return banks
+
+        def quantise_weights(w, banks):
+            grouped = weight_pool.tile([P, OUTS * PACK], BF16, align_bytes=64)
+            grouped_words = grouped[:].bitcast(F32).rearrange("q (o u) -> q o u", u=2)
+            for half, bank in enumerate(banks):
                 nc.vector.tensor_copy(
-                    out=grouped_words[:, w, half * 2 * P : (half + 1) * 2 * P, :],
+                    out=grouped_words[:, half * 2 * P : (half + 1) * 2 * P, :],
                     in_=bank[:].rearrange("q u o -> q o u"),
                 )
             codes, scales = weight_pass(w)
-            nc.vector.quantize_mx(
-                out=codes, scales=scales, in_=w_grouped[:, w * OUTS * PACK : (w + 1) * OUTS * PACK]
-            )
+            nc.vector.quantize_mx(out=codes, scales=scales, in_=grouped[:])
 
         nc.vector.memset(minus_quarter[:], -0.25)
         nc.scalar.activation(out=warm[:], in_=minus_quarter[:], func=FUNC.Silu)
@@ -202,31 +207,37 @@ def tile_kan1_pa_t_kernel(tc, x, fc1_spline_w, fc1_base_w, fc1_base_b, out):
 
         for n in range(UNITS_PER_BATCH):
             load_x_block(n)
-        for b in range(1, BATCH):
+        for b in range(1, FIRST_WEIGHT_BATCH + 1):
             load_x(b)
         nc.sync.dma_start(out=ws_raw[:].rearrange("o (ob k) -> o ob k", ob=4),
                           in_=fc1_spline_w.rearrange("(ob o) k -> o ob k", o=P))
         nc.sync.dma_start(out=wb_raw[:].rearrange("o (ob k) -> o ob k", ob=4),
                           in_=fc1_base_w.rearrange("(ob o) k -> o ob k", o=P))
         nc.sync.dma_start(out=bias_bf[:], in_=fc1_base_b.partition_broadcast(P))
+        for b in range(FIRST_WEIGHT_BATCH + 1, BATCH):
+            load_x(b)
 
         squares_of = {}
         quarters = {n: quarter(n) for n in range(2)}
         silu_waiting = None
+        banks_waiting = None
         for b in range(BATCH + 1):
-            for n in range(b * LEAD // BATCH, min((b + 1) * LEAD // BATCH, LEAD)):
+            for n in range(max(2 * b - 1, 0), min(2 * b + 1, LEAD)):
                 squares_of[n] = square(n, quarters[n])
                 quarters[n + 2] = quarter(n + 2)
             if silu_waiting is not None:
                 quantise_silu(b - 1, silu_waiting, 0, 2 * UNIT_C)
                 quantise_silu(b - 1, silu_waiting, 2 * UNIT_C, UNIT_C)
+            if banks_waiting is not None:
+                quantise_weights(b - 1 - FIRST_WEIGHT_BATCH, banks_waiting)
+                banks_waiting = None
             if b == BATCH:
                 break
-            silu_waiting = silu_pool.tile([P, CHANNELS * PACK], BF16, align_bytes=64)
+            silu_waiting = bf16_pool.tile([P, CHANNELS * PACK], BF16, name="silu_bf", tag="bf16", align_bytes=64)
             for first in range(0, CHANNELS, UNIT_C if b == 0 else CHANNELS):
                 silu(b, silu_waiting, first, UNIT_C if b == 0 else CHANNELS)
-            if b >= FIRST_WEIGHT_BATCH:
-                prepare_weights(b - FIRST_WEIGHT_BATCH)
+            if 0 <= b - FIRST_WEIGHT_BATCH < WEIGHT_PASSES:
+                banks_waiting = transpose_weights(b - FIRST_WEIGHT_BATCH)
         nc.vector.tensor_copy(out=bias_f32[:], in_=bias_bf[:])
 
         waiting = None

from contextlib import ExitStack

import concourse.mybir as mybir
from concourse.masks import make_identity

F32 = mybir.dt.float32
BF16 = mybir.dt.bfloat16
U32 = mybir.dt.uint32
U8 = mybir.dt.uint8
FP8X4 = mybir.dt.float8_e4m3fn_x4
FUNC = mybir.ActivationFunctionType
ALU = mybir.AluOpType

BATCH, PATCHES, CHANNELS, OUTS = 8, 512, 768, 512
P = 128
PACK = 4
ROWS = PATCHES // P
UNIT_C = 256
C_TILES = UNIT_C // P
UNITS_PER_BATCH = CHANNELS // UNIT_C
UNITS = BATCH * UNITS_PER_BATCH
SPLINE_PASSES = 2
BASE_PASS = 2
WEIGHT_PASSES = SPLINE_PASSES + 1
LEAD = 11
FIRST_WEIGHT_BATCH = 4

FLOPS = 2 * BATCH * CHANNELS * OUTS * (2 * PATCHES + PATCHES)


def tile_kan1_pa_t_kernel(tc, x, fc1_spline_w, fc1_base_w, fc1_base_b, out):
    nc = tc.nc
    with ExitStack() as ctx:
        keep = ctx.enter_context(tc.tile_pool(name="keep", bufs=1))
        bf16_pool = ctx.enter_context(tc.tile_pool(name="bf16_pool", bufs=3))
        weight_pool = ctx.enter_context(tc.tile_pool(name="weight_pool", bufs=1))
        square_pool = ctx.enter_context(tc.tile_pool(name="square_pool", bufs=LEAD + 1))
        basis_pool = ctx.enter_context(tc.tile_pool(name="basis_pool", bufs=3))
        result_pool = ctx.enter_context(tc.tile_pool(name="result_pool", bufs=4))
        psum_quarter = ctx.enter_context(tc.psum_pool(name="psum_quarter", bufs=2))
        psum_acc = ctx.enter_context(tc.psum_pool(name="psum_acc", bufs=6))
        ctx.enter_context(tc.manual_schedule())

        x_sb = [keep.tile([P, ROWS * CHANNELS], BF16, name="x_sb%d" % b) for b in range(BATCH)]
        ws_raw = keep.tile([P, 4 * 2 * PATCHES], BF16)
        wb_raw = keep.tile([P, 4 * PATCHES], BF16)
        w_codes = keep.tile([P, WEIGHT_PASSES * OUTS], U32, align_bytes=64)
        w_scales = keep.tile([P, WEIGHT_PASSES * OUTS], U8, align_bytes=64)
        silu_codes = keep.tile([P, UNITS * UNIT_C], U32, align_bytes=64)
        silu_scales = keep.tile([P, UNITS * UNIT_C], U8, align_bytes=64)
        bias_bf = keep.tile([P, OUTS], BF16)
        bias_f32 = keep.tile([P, OUTS], F32)
        identity = keep.tile([P, P], F32)
        quarter_identity = keep.tile([P, P], BF16)
        minus_quarter = keep.tile([P, 1], F32)
        warm = keep.tile([P, 1], F32)

        def x_block(n):
            b, cb = divmod(n, UNITS_PER_BATCH)
            rows = x_sb[b][:].rearrange("q (r c) -> q r c", r=ROWS)
            return rows[:, :, cb * UNIT_C : (cb + 1) * UNIT_C]

        def load_x(b):
            nc.sync.dma_start(
                out=x_sb[b][:].rearrange("q (g r) -> q g r", g=2),
                in_=x[b].rearrange("(g q j) c -> q g (j c)", g=2, j=2),
            )

        def load_x_block(n):
            b, cb = divmod(n, UNITS_PER_BATCH)
            for g in range(2):
                nc.sync.dma_start(
                    out=x_block(n)[:, 2 * g : 2 * g + 2, :],
                    in_=x[b, g * 2 * P : (g + 1) * 2 * P, cb * UNIT_C : (cb + 1) * UNIT_C].rearrange(
                        "(q j) c -> q j c", j=2
                    ),
                )

        def silu(b, silu_bf, first, width):
            rows = x_sb[b][:].rearrange("q (r c) -> q r c", r=ROWS)[:, :, first : first + width]
            nc.scalar.activation(
                out=silu_bf[:, first * PACK : (first + width) * PACK].rearrange("q (s i r) -> q s r i", i=4, r=ROWS),
                in_=rows.rearrange("q r (s i) -> q s r i", i=4),
                func=FUNC.Silu,
            )

        def quantise_silu(b, silu_bf, first, width):
            cols = slice(b * CHANNELS + first, b * CHANNELS + first + width)
            nc.vector.quantize_mx(
                out=silu_codes[:, cols].bitcast(FP8X4),
                scales=silu_scales[:, cols],
                in_=silu_bf[:, first * PACK : (first + width) * PACK],
            )

        def quarter(n):
            bank = psum_quarter.tile([P, ROWS, UNIT_C], BF16)
            for half in range(2):
                rows = slice(2 * half, 2 * half + 2)
                nc.tensor.matmul(
                    out=bank[:, rows, :], lhsT=quarter_identity[:], rhs=x_block(n)[:, rows, :], start=True, stop=True
                )
            return bank

        def square(n, bank):
            squares = square_pool.tile([P, ROWS * 2 * UNIT_C], F32)
            planes = squares[:].rearrange("q (r i c) -> q r i c", r=ROWS, i=2)
            nc.vector.scalar_tensor_tensor(
                out=planes[:, :, 0, :], in0=x_block(n), scalar=2.0, in1=bank[:], op0=ALU.add, op1=ALU.mult
            )
            nc.gpsimd.tensor_tensor(out=planes[:, :, 1, :], in0=planes[:, :, 0, :], in1=x_block(n), op=ALU.subtract)
            return squares

        def exp_basis(squares):
            basis_bf = bf16_pool.tile([P, SPLINE_PASSES * UNIT_C * PACK], BF16, name="basis_bf", tag="bf16", align_bytes=64)
            src = squares[:].rearrange("q (g t s i) -> q g s t i", g=SPLINE_PASSES, t=PACK, i=4)
            dst = basis_bf[:].rearrange("q (g s i t) -> q g s t i", g=SPLINE_PASSES, t=PACK, i=4)
            for g in range(SPLINE_PASSES):
                nc.scalar.activation(
                    out=dst[:, g], in_=src[:, g], func=FUNC.Exp, scale=-1.0, bias=minus_quarter[:]
                )
            return basis_bf

        def quantise_basis(basis_bf):
            basis_codes = basis_pool.tile([P, SPLINE_PASSES * UNIT_C], U32, align_bytes=64)
            basis_scales = basis_pool.tile([P, SPLINE_PASSES * UNIT_C], U8, align_bytes=64)
            nc.vector.quantize_mx(out=basis_codes[:].bitcast(FP8X4), scales=basis_scales[:], in_=basis_bf[:])
            return basis_codes, basis_scales

        def weight_pass(w):
            cols = slice(w * OUTS, (w + 1) * OUTS)
            return w_codes[:, cols].bitcast(FP8X4), w_scales[:, cols]

        def multiply(n, basis_codes, basis_scales):
            sums = [psum_acc.tile([P, OUTS], F32, name="acc%d" % ct, tag="acc") for ct in range(C_TILES)]
            rhs, rhs_scale = weight_pass(BASE_PASS)
            for ct in range(C_TILES):
                cols = slice(n * UNIT_C + ct * P, n * UNIT_C + (ct + 1) * P)
                nc.tensor.matmul_mx(
                    out=sums[ct][:],
                    lhsT=silu_codes[:, cols].bitcast(FP8X4),
                    lhsT_scale=silu_scales[:, cols],
                    rhs=rhs,
                    rhs_scale=rhs_scale,
                    start=True,
                    stop=False,
                )
            for g in range(SPLINE_PASSES):
                rhs, rhs_scale = weight_pass(g)
                for ct in range(C_TILES):
                    cols = slice(g * UNIT_C + ct * P, g * UNIT_C + (ct + 1) * P)
                    nc.tensor.matmul_mx(
                        out=sums[ct][:],
                        lhsT=basis_codes[:, cols].bitcast(FP8X4),
                        lhsT_scale=basis_scales[:, cols],
                        rhs=rhs,
                        rhs_scale=rhs_scale,
                        start=False,
                        stop=(g == SPLINE_PASSES - 1),
                    )
            return sums

        def add_bias_and_store(n, sums):
            b, cb = divmod(n, UNITS_PER_BATCH)
            for ct in range(C_TILES):
                result = result_pool.tile([P, OUTS], F32)
                nc.vector.tensor_tensor(out=result[:], in0=sums[ct][:], in1=bias_f32[:], op=ALU.add)
                first = cb * UNIT_C + ct * P
                nc.sync.dma_start(out=out[b, first : first + P, :], in_=result[:])

        def transpose_weights(w):
            if w == BASE_PASS:
                words = wb_raw[:].bitcast(F32).rearrange("o (ob k) -> o ob k", ob=4)
            else:
                words = ws_raw[:].bitcast(F32).rearrange("o (ob k) -> o ob k", ob=4)
            banks = []
            for half in range(2):
                bank = psum_acc.tile([P, 2, 2 * P], F32, name="w_bank%d" % half, tag="acc")
                for u in range(2):
                    if w == BASE_PASS:
                        picked = slice(u * P, (u + 1) * P)
                    else:
                        picked = slice(w * 2 * P + u, (w + 1) * 2 * P, 2)
                    for ob in range(2):
                        nc.tensor.transpose(
                            bank[:, u, ob * P : (ob + 1) * P], words[:, 2 * half + ob, picked], identity[:]
                        )
                banks.append(bank)
            return banks

        def quantise_weights(w, banks):
            grouped = weight_pool.tile([P, OUTS * PACK], BF16, align_bytes=64)
            grouped_words = grouped[:].bitcast(F32).rearrange("q (o u) -> q o u", u=2)
            for half, bank in enumerate(banks):
                nc.vector.tensor_copy(
                    out=grouped_words[:, half * 2 * P : (half + 1) * 2 * P, :],
                    in_=bank[:].rearrange("q u o -> q o u"),
                )
            codes, scales = weight_pass(w)
            nc.vector.quantize_mx(out=codes, scales=scales, in_=grouped[:])

        nc.vector.memset(minus_quarter[:], -0.25)
        nc.scalar.activation(out=warm[:], in_=minus_quarter[:], func=FUNC.Silu)
        make_identity(nc, identity[:])
        nc.vector.tensor_scalar(
            out=quarter_identity[:], in0=identity[:], scalar1=0.25, scalar2=None, op0=ALU.mult
        )

        for n in range(UNITS_PER_BATCH):
            load_x_block(n)
        for b in range(1, FIRST_WEIGHT_BATCH + 1):
            load_x(b)
        nc.sync.dma_start(out=ws_raw[:].rearrange("o (ob k) -> o ob k", ob=4),
                          in_=fc1_spline_w.rearrange("(ob o) k -> o ob k", o=P))
        nc.sync.dma_start(out=wb_raw[:].rearrange("o (ob k) -> o ob k", ob=4),
                          in_=fc1_base_w.rearrange("(ob o) k -> o ob k", o=P))
        nc.sync.dma_start(out=bias_bf[:], in_=fc1_base_b.partition_broadcast(P))
        for b in range(FIRST_WEIGHT_BATCH + 1, BATCH):
            load_x(b)

        squares_of = {}
        quarters = {n: quarter(n) for n in range(2)}
        silu_waiting = None
        banks_waiting = None
        for b in range(BATCH + 1):
            for n in range(max(2 * b - 1, 0), min(2 * b + 1, LEAD)):
                squares_of[n] = square(n, quarters[n])
                quarters[n + 2] = quarter(n + 2)
            if silu_waiting is not None:
                quantise_silu(b - 1, silu_waiting, 0, 2 * UNIT_C)
                quantise_silu(b - 1, silu_waiting, 2 * UNIT_C, UNIT_C)
            if banks_waiting is not None:
                quantise_weights(b - 1 - FIRST_WEIGHT_BATCH, banks_waiting)
                banks_waiting = None
            if b == BATCH:
                break
            silu_waiting = bf16_pool.tile([P, CHANNELS * PACK], BF16, name="silu_bf", tag="bf16", align_bytes=64)
            for first in range(0, CHANNELS, UNIT_C if b == 0 else CHANNELS):
                silu(b, silu_waiting, first, UNIT_C if b == 0 else CHANNELS)
            if 0 <= b - FIRST_WEIGHT_BATCH < WEIGHT_PASSES:
                banks_waiting = transpose_weights(b - FIRST_WEIGHT_BATCH)
        nc.vector.tensor_copy(out=bias_f32[:], in_=bias_bf[:])

        waiting = None
        for n in range(UNITS):
            if n + LEAD < UNITS:
                squares_of[n + LEAD] = square(n + LEAD, quarters[n + LEAD])
            if n + LEAD + 2 < UNITS:
                quarters[n + LEAD + 2] = quarter(n + LEAD + 2)
            basis_bf = exp_basis(squares_of[n])
            basis_codes, basis_scales = quantise_basis(basis_bf)
            sums = multiply(n, basis_codes, basis_scales)
            if waiting is not None:
                add_bias_and_store(n - 1, waiting)
            waiting = sums
        add_bias_and_store(UNITS - 1, waiting)
